import numpy as np
import ml_dtypes


def mxq(x, axis, fmt="e4m3"):
    dtype, down = {"e4m3": (ml_dtypes.float8_e4m3fn, 7), "e5m2": (ml_dtypes.float8_e5m2, 14)}[fmt]
    v = np.moveaxis(np.asarray(x, np.float32).astype(ml_dtypes.bfloat16).astype(np.float64), axis, -1)
    blocks = v.reshape(v.shape[:-1] + (-1, 32))
    amax = np.abs(blocks).max(-1, keepdims=True)
    byte = np.maximum(np.where(amax > 0, np.frexp(amax)[1] - 1 + 127, 0) - down, 1)
    scale = np.exp2(byte - 127.0)
    codes = (blocks / scale).astype(np.float32).astype(dtype).astype(np.float64)
    return np.moveaxis((codes * scale).reshape(v.shape), -1, axis)


WIDE = False


def mx_kscale(k):
    if not WIDE:
        return np.ones(k)
    levels = np.array([30, -30])
    if k % 512:
        return np.exp2(np.random.permutation(np.resize(levels, k // 32))).repeat(32)
    a = np.empty((k // 512, 16))
    for p in range(k // 512):
        a[p, :8] = np.random.permutation(np.resize(levels, 8))
        for g in range(8):
            far = levels[np.abs(levels - a[p, g]) >= 10]
            a[p, g + 8] = far[np.random.randint(len(far))]
    return np.exp2(a.ravel()).repeat(32)


BF16 = ml_dtypes.bfloat16


def bf(x):
    return np.asarray(x, np.float32).astype(BF16)


def f64(x):
    return np.asarray(x).astype(np.float64)


B, S, HID, NH, DH = 4, 256, 1024, 16, 64
DQ = NH * DH


def setup_inputs():
    s = mx_kscale(HID)

    def w():
        return bf(np.random.standard_normal((HID, DQ)) / np.sqrt(HID) / s[:, None])

    def b():
        return bf(np.random.standard_normal(DQ) * 0.3)

    return {"x": bf(np.random.standard_normal((B, S, HID)) * s),
            "reasoning_mask": bf(np.random.uniform(size=(B, S, 1, 1))),
            "Wq": w(), "bq": b(), "Wk": w(), "bk": b(),
            "Wqr": w(), "bqr": b(), "Wkr": w(), "bkr": b()}


def reference(x, reasoning_mask, Wq, bq, Wk, bk, Wqr, bqr, Wkr, bkr):
    xq = mxq(f64(x), 2, "e5m2")
    g = f64(reasoning_mask)

    def proj(W, b):
        return ((xq @ mxq(f64(W), 0, "e5m2")) + f64(b)).reshape(B, S, NH, DH)

    q = proj(Wq, bq)
    k = proj(Wk, bk)
    q_r = proj(Wqr, bqr)
    k_r = proj(Wkr, bkr)
    q = q * (1.0 - g) + q_r * g
    k = k * (1.0 - g) + k_r * g
    return q, k

@@ -1,0 +1,271 @@
+from contextlib import ExitStack
+
+import concourse.mybir as mybir
+from concourse.masks import make_identity
+
+B, S, HID, NH, DH = 4, 256, 1024, 16, 64
+TOKENS = B * S
+DQ = NH * DH
+FLOPS = 4 * 2 * TOKENS * HID * DQ
+
+F32 = mybir.dt.float32
+BF16 = mybir.dt.bfloat16
+U32 = mybir.dt.uint32
+U8 = mybir.dt.uint8
+E5M2X4 = mybir.dt.float8_e5m2_x4
+MULT = mybir.AluOpType.mult
+ADD = mybir.AluOpType.add
+
+P = 128
+PACK = 4
+K_PASS = P * PACK
+PASSES = HID // K_PASS
+N_TILE = 512
+TILES = TOKENS // P
+HALVES = DQ // N_TILE
+STAGES = 2 * HALVES
+CHUNKS = 2 * STAGES
+VECTOR_COLS = 256
+LEAD = 5
+QJ = 4
+
+
+def tile_reasoningmultiheadattention_pa_kernel(
+    tc, x, reasoning_mask, Wq, bq, Wk, bk, Wqr, bqr, Wkr, bkr, out_0, out_1
+):
+    nc = tc.nc
+    x_rows = x.rearrange("b s k -> (b s) k").rearrange("(p j) k -> p j k", j=TILES)
+    gate = reasoning_mask.rearrange("b s u v -> (b s u v)")
+    out_rows = [
+        o.rearrange("b s h d -> (b s) (h d)").rearrange("(p j) n -> p j n", j=TILES)
+        for o in (out_0, out_1)
+    ]
+    weights = [(Wq, Wqr), (Wk, Wkr)]
+    biases = [(bq, bqr), (bk, bkr)]
+
+    with ExitStack() as ctx:
+        keep = ctx.enter_context(tc.tile_pool(name="keep", bufs=1))
+        x_stage = ctx.enter_context(tc.tile_pool(name="x_stage", bufs=2))
+        w_stage = ctx.enter_context(tc.tile_pool(name="w_stage", bufs=3))
+        acc_pool = ctx.enter_context(tc.tile_pool(name="acc", bufs=24))
+        mx_psum = ctx.enter_context(tc.psum_pool(name="mx_psum", bufs=5))
+        plain_psum = ctx.enter_context(tc.psum_pool(name="plain_psum", bufs=3))
+        ctx.enter_context(tc.manual_schedule())
+
+        ident = keep.tile([P, P], F32, name="ident")
+        gate_raw = keep.tile([P, TOKENS], BF16, name="gate_raw")
+        gate_rows = keep.tile([P, TILES, P], BF16, name="gate_rows")
+        gate_col_raw = keep.tile([P, TILES], BF16, name="gate_col_raw")
+        gate_col = keep.tile([P, TILES], F32, name="gate_col")
+        one_minus_gate = keep.tile([P, TILES], F32, name="one_minus_gate")
+        bias_rows = [keep.tile([P, DQ], BF16, name="bias_rows%d" % o) for o in range(2)]
+        x_raw = [keep.tile([P, 2, HID], BF16, name="x_raw%d" % a) for a in range(TILES // 2)]
+        x_codes = [keep.tile([P, 2 * PASSES * P], U32, name="x_codes%d" % a, align_bytes=64) for a in range(TILES // 2)]
+        x_scales = [keep.tile([P, 2 * PASSES * P], U8, name="x_scales%d" % a, align_bytes=64) for a in range(TILES // 2)]
+        w_raw = [
+            [keep.tile([P, PACK, N_TILE], BF16, name="w_raw%d_%d" % (h, g)) for g in range(PASSES)]
+            for h in range(CHUNKS)
+        ]
+        x_grouped, w_grouped, w_codes, w_scales, acc, banks, x_banks, bias_banks = {}, {}, {}, {}, {}, {}, {}, {}
+
+        def out_cols(s):
+            return slice((s % HALVES) * N_TILE, (s % HALVES + 1) * N_TILE)
+
+        def load_biases(queue, o):
+            plain, gated = biases[o]
+            queue.dma_start(out=bias_rows[o][0:1, :], in_=gated.partition_broadcast(1))
+            queue.dma_start(out=bias_rows[o][32:96:32, :], in_=plain.partition_broadcast(2))
+
+        def load_x(a):
+            nc.sync.dma_start(out=x_raw[a][:], in_=x_rows[:, 2 * a : 2 * a + 2, :])
+
+        def load_w(h, g):
+            s = h // 2
+            rows = weights[s // HALVES][h % 2][g * K_PASS : (g + 1) * K_PASS, out_cols(s)]
+            nc.sync.dma_start(out=w_raw[h][g][:], in_=rows.rearrange("(p t) n -> p t n", t=PACK))
+
+        def transpose_x(j):
+            x_banks[j] = plain_psum.tile([P, PASSES, 2, P], F32, name="plain", tag="plain")
+            words = x_raw[j // 2][:, j % 2, :].bitcast(F32)
+            for g in range(PASSES):
+                for u in range(2):
+                    nc.tensor.transpose(x_banks[j][:, g, u, :], words[:, 256 * g + u : 256 * (g + 1) : 2], ident[:])
+
+        def group_x(copy, j):
+            if j % 2 == 0:
+                x_grouped[j // 2] = x_stage.tile([P, 2, PASSES, P, PACK], BF16, name="x_grouped", align_bytes=64)
+            copy(out=x_grouped[j // 2][:, j % 2].bitcast(F32), in_=x_banks[j][:].rearrange("p g u r -> p g r u"))
+
+        def quantize_x(a):
+            nc.vector.quantize_mx(
+                out=x_codes[a][:].bitcast(E5M2X4),
+                scales=x_scales[a][:],
+                in_=x_grouped[a][:].rearrange("p i g r t -> p (i g r t)"),
+            )
+
+        def group_w(copy, h, g, n0, n1):
+            if h not in w_grouped:
+                w_grouped[h] = w_stage.tile([P, PASSES, N_TILE, PACK], BF16, name="w_grouped", align_bytes=64)
+            copy(
+                out=w_grouped[h][:, g, n0:n1, :].rearrange("p (c i) t -> p c t i", i=4),
+                in_=w_raw[h][g][:, :, n0:n1].rearrange("p t (c i) -> p c t i", i=4),
+            )
+
+        def quantize_w(h, g0, g1):
+            if h not in w_codes:
+                w_codes[h] = w_stage.tile([P, PASSES * N_TILE], U32, name="w_codes", align_bytes=64)
+                w_scales[h] = w_stage.tile([P, PASSES * N_TILE], U8, name="w_scales", align_bytes=64)
+            cols = slice(g0 * N_TILE, g1 * N_TILE)
+            nc.vector.quantize_mx(
+                out=w_codes[h][:, cols].bitcast(E5M2X4),
+                scales=w_scales[h][:, cols],
+                in_=w_grouped[h][:, g0:g1].rearrange("p g n t -> p (g n t)"),
+            )
+
+        def blend_bias(s, j):
+            bias_banks[s, j] = plain_psum.tile([P, N_TILE], F32, name="plain", tag="plain")
+            nc.tensor.matmul(
+                out=bias_banks[s, j][:],
+                lhsT=gate_rows[:, j, :],
+                rhs=bias_rows[s // HALVES][:, out_cols(s)],
+                start=True,
+                stop=True,
+            )
+
+        def start_acc(copy, s, j):
+            acc[s, j] = acc_pool.tile([P, N_TILE], F32, name="acc")
+            copy(out=acc[s, j][:], in_=bias_banks[s, j][:])
+
+        def mx_pass(h, j, g):
+            if g == 0:
+                banks[h, j] = mx_psum.tile([P, N_TILE], F32, name="mx")
+            x_cols = slice(((j % 2) * PASSES + g) * P, ((j % 2) * PASSES + g + 1) * P)
+            w_cols = slice(g * N_TILE, (g + 1) * N_TILE)
+            nc.tensor.matmul_mx(
+                out=banks[h, j][:],
+                lhsT=x_codes[j // 2][:, x_cols].bitcast(E5M2X4),
+                lhsT_scale=x_scales[j // 2][:, x_cols],
+                rhs=w_codes[h][:, w_cols].bitcast(E5M2X4),
+                rhs_scale=w_scales[h][:, w_cols],
+                start=(g == 0),
+                stop=(g == PASSES - 1),
+            )
+
+        def project(h, j):
+            for g in range(PASSES):
+                mx_pass(h, j, g)
+
+        def blend(h, j):
+            s = h // 2
+            factor = (one_minus_gate, gate_col)[h % 2]
+            nc.vector.scalar_tensor_tensor(
+                out=acc[s, j][:], in0=banks[h, j][:], scalar=factor[:, j : j + 1], in1=acc[s, j][:], op0=MULT, op1=ADD
+            )
+            if h % 2 == 1:
+                nc.sync.dma_start(out=out_rows[s // HALVES][:, j, out_cols(s)], in_=acc[s, j][:])
+
+        on_vector = nc.vector.tensor_copy
+        on_scalar = nc.scalar.copy
+
+        for o in range(2):
+            nc.vector.memset(bias_rows[o][:], 0.0)
+        make_identity(nc, ident[:])
+        nc.gpsimd.memset(gate_rows[:], 1.0)
+        nc.scalar.dma_start(out=gate_raw[0:128:64, :], in_=gate.partition_broadcast(2))
+        nc.scalar.dma_start(out=gate_col_raw[:], in_=gate.rearrange("(p j) -> p j", j=TILES))
+        load_biases(nc.scalar, 0)
+        load_x(0)
+        load_w(0, 0)
+        load_x(1)
+        load_w(0, 1)
+        load_x(2)
+        load_x(3)
+        for h in range(1, CHUNKS):
+            for g in range(PASSES):
+                load_w(h, g)
+            if h == 1:
+                load_biases(nc.sync, 1)
+
+        nc.scalar.copy(out=gate_rows[0:1], in_=gate_raw[0:1, :].rearrange("p (m j) -> p j m", j=TILES))
+        nc.vector.tensor_scalar(
+            out=gate_rows[64:65], in0=gate_raw[64:65, :].rearrange("p (m j) -> p j m", j=TILES),
+            scalar1=-1.0, scalar2=None, op0=MULT,
+        )
+        nc.vector.tensor_scalar(
+            out=one_minus_gate[:], in0=gate_col_raw[:], scalar1=-1.0, scalar2=1.0, op0=MULT, op1=ADD
+        )
+        nc.vector.tensor_copy(out=gate_col[:], in_=gate_col_raw[:])
+
+        def bias(copy, q):
+            blend_bias(*divmod(q, TILES))
+            start_acc(copy, *divmod(q, TILES))
+
+        transpose_x(0)
+        group_x(on_vector, 0)
+        transpose_x(1)
+        group_x(on_scalar, 1)
+        group_w(on_vector, 0, 0, 0, N_TILE)
+        bias(on_scalar, 0)
+        bias(on_scalar, 1)
+        quantize_x(0)
+        quantize_w(0, 0, 1)
+        for j in range(2, 4):
+            transpose_x(j)
+            group_x(on_scalar, j)
+        group_w(on_vector, 0, 1, 0, N_TILE)
+        quantize_x(1)
+        quantize_w(0, 1, 2)
+        bias(on_scalar, 2)
+        bias(on_scalar, 3)
+        for j in range(2):
+            mx_pass(0, j, 0)
+        for j in range(4, TILES):
+            transpose_x(j)
+            group_x(on_scalar, j)
+            if j == 5:
+                for j2 in range(2):
+                    mx_pass(0, j2, 1)
+        project(0, 2)
+        project(0, 3)
+        blend(0, 0)
+        quantize_x(2)
+        blend(0, 1)
+        quantize_x(3)
+        group_w(on_vector, 1, 0, 0, N_TILE)
+        bias(on_scalar, 4)
+        bias(on_scalar, 5)
+        group_w(on_scalar, 1, 1, 0, N_TILE)
+        project(0, 4)
+        project(0, 5)
+        bias(on_scalar, 6)
+        project(0, 6)
+        bias(on_scalar, 7)
+        blend(0, 2)
+        project(0, 7)
+        blend(0, 3)
+        quantize_w(1, 0, 1)
+        blend(0, 4)
+        blend(0, 5)
+        quantize_w(1, 1, 2)
+        blend(0, 6)
+        blend(0, 7)
+        group_w(on_scalar, 2, 0, 0, N_TILE)
+        for q in range(TILES, 4 + LEAD):
+            bias(on_scalar, q)
+
+        for h in range(1, CHUNKS):
+            for j in range(TILES):
+                q = 4 * h + LEAD + j // 2
+                if j % 2 == 0 and q < STAGES * TILES:
+                    bias(on_scalar, q)
+                project(h, j)
+                blend(h, j)
+                if h + 1 < CHUNKS:
+                    if j == 0:
+                        group_w(on_scalar, h + 1, 1, VECTOR_COLS, N_TILE)
+                    if j == 1:
+                        group_w(on_vector, h + 1, 1, 0, VECTOR_COLS)
+                    if j == QJ:
+                        quantize_w(h + 1, 0, PASSES)
+                if j in (2, 4) and h + 2 < CHUNKS:
+                    group_w(on_scalar, h + 2, 0, (j - 2) * 128, j * 128)

@@ -15,6 +15,7 @@ U8 = mybir.dt.uint8
 E5M2X4 = mybir.dt.float8_e5m2_x4
 MULT = mybir.AluOpType.mult
 ADD = mybir.AluOpType.add
+COPY = mybir.ActivationFunctionType.Copy
 
 P = 128
 PACK = 4
@@ -25,9 +26,12 @@ TILES = TOKENS // P
 HALVES = DQ // N_TILE
 STAGES = 2 * HALVES
 CHUNKS = 2 * STAGES
-VECTOR_COLS = 256
-LEAD = 5
-QJ = 4
+VECTOR_COLS = 160
+LEAD = 3
+LAG = 4
+AHEAD = 4
+QS = 1
+OFF_VECTOR = ((6, 4), (6, 5), (6, 6), (6, 7))
 
 
 def tile_reasoningmultiheadattention_pa_kernel(
@@ -45,11 +49,10 @@ def tile_reasoningmultiheadattention_pa_kernel(
 
     with ExitStack() as ctx:
         keep = ctx.enter_context(tc.tile_pool(name="keep", bufs=1))
-        x_stage = ctx.enter_context(tc.tile_pool(name="x_stage", bufs=2))
-        w_stage = ctx.enter_context(tc.tile_pool(name="w_stage", bufs=3))
+        x_stage = ctx.enter_context(tc.tile_pool(name="x_stage", bufs=3))
+        w_stage = ctx.enter_context(tc.tile_pool(name="w_stage", bufs=4))
         acc_pool = ctx.enter_context(tc.tile_pool(name="acc", bufs=24))
-        mx_psum = ctx.enter_context(tc.psum_pool(name="mx_psum", bufs=5))
-        plain_psum = ctx.enter_context(tc.psum_pool(name="plain_psum", bufs=3))
+        psum = ctx.enter_context(tc.psum_pool(name="psum", bufs=8))
         ctx.enter_context(tc.manual_schedule())
 
         ident = keep.tile([P, P], F32, name="ident")
@@ -85,7 +88,7 @@ def tile_reasoningmultiheadattention_pa_kernel(
             nc.sync.dma_start(out=w_raw[h][g][:], in_=rows.rearrange("(p t) n -> p t n", t=PACK))
 
         def transpose_x(j):
-            x_banks[j] = plain_psum.tile([P, PASSES, 2, P], F32, name="plain", tag="plain")
+            x_banks[j] = psum.tile([P, PASSES, 2, P], F32, name="bank")
             words = x_raw[j // 2][:, j % 2, :].bitcast(F32)
             for g in range(PASSES):
                 for u in range(2):
@@ -123,7 +126,7 @@ def tile_reasoningmultiheadattention_pa_kernel(
             )
 
         def blend_bias(s, j):
-            bias_banks[s, j] = plain_psum.tile([P, N_TILE], F32, name="plain", tag="plain")
+            bias_banks[s, j] = psum.tile([P, N_TILE], F32, name="bank")
             nc.tensor.matmul(
                 out=bias_banks[s, j][:],
                 lhsT=gate_rows[:, j, :],
@@ -138,7 +141,7 @@ def tile_reasoningmultiheadattention_pa_kernel(
 
         def mx_pass(h, j, g):
             if g == 0:
-                banks[h, j] = mx_psum.tile([P, N_TILE], F32, name="mx")
+                banks[h, j] = psum.tile([P, N_TILE], F32, name="bank")
             x_cols = slice(((j % 2) * PASSES + g) * P, ((j % 2) * PASSES + g + 1) * P)
             w_cols = slice(g * N_TILE, (g + 1) * N_TILE)
             nc.tensor.matmul_mx(
@@ -157,10 +160,15 @@ def tile_reasoningmultiheadattention_pa_kernel(
 
         def blend(h, j):
             s = h // 2
-            factor = (one_minus_gate, gate_col)[h % 2]
-            nc.vector.scalar_tensor_tensor(
-                out=acc[s, j][:], in0=banks[h, j][:], scalar=factor[:, j : j + 1], in1=acc[s, j][:], op0=MULT, op1=ADD
-            )
+            factor = (one_minus_gate, gate_col)[h % 2][:, j : j + 1]
+            if (h, j) in OFF_VECTOR:
+                scaled = x_stage.tile([P, N_TILE], F32, name="scaled", bufs=3)
+                nc.scalar.activation(out=scaled[:], in_=banks[h, j][:], func=COPY, scale=factor)
+                nc.gpsimd.tensor_tensor(out=acc[s, j][:], in0=acc[s, j][:], in1=scaled[:], op=ADD)
+            else:
+                nc.vector.scalar_tensor_tensor(
+                    out=acc[s, j][:], in0=banks[h, j][:], scalar=factor, in1=acc[s, j][:], op0=MULT, op1=ADD
+                )
             if h % 2 == 1:
                 nc.sync.dma_start(out=out_rows[s // HALVES][:, j, out_cols(s)], in_=acc[s, j][:])
 
@@ -174,8 +182,8 @@ def tile_reasoningmultiheadattention_pa_kernel(
         nc.scalar.dma_start(out=gate_raw[0:128:64, :], in_=gate.partition_broadcast(2))
         nc.scalar.dma_start(out=gate_col_raw[:], in_=gate.rearrange("(p j) -> p j", j=TILES))
         load_biases(nc.scalar, 0)
-        load_x(0)
         load_w(0, 0)
+        load_x(0)
         load_x(1)
         load_w(0, 1)
         load_x(2)
@@ -186,86 +194,86 @@ def tile_reasoningmultiheadattention_pa_kernel(
             if h == 1:
                 load_biases(nc.sync, 1)
 
-        nc.scalar.copy(out=gate_rows[0:1], in_=gate_raw[0:1, :].rearrange("p (m j) -> p j m", j=TILES))
-        nc.vector.tensor_scalar(
-            out=gate_rows[64:65], in0=gate_raw[64:65, :].rearrange("p (m j) -> p j m", j=TILES),
-            scalar1=-1.0, scalar2=None, op0=MULT,
-        )
-        nc.vector.tensor_scalar(
-            out=one_minus_gate[:], in0=gate_col_raw[:], scalar1=-1.0, scalar2=1.0, op0=MULT, op1=ADD
-        )
+        nc.scalar.activation(out=one_minus_gate[:], in_=gate_col_raw[:], func=COPY, scale=-1.0, bias=1.0)
+        tile_major = gate_raw[:].rearrange("p (m j) -> p j m", j=TILES)
+        nc.scalar.copy(out=gate_rows[0:1, 0:4], in_=tile_major[0:1, 0:4])
+        nc.vector.tensor_scalar(out=gate_rows[64:65], in0=tile_major[64:65], scalar1=-1.0, scalar2=None, op0=MULT)
         nc.vector.tensor_copy(out=gate_col[:], in_=gate_col_raw[:])
+        nc.scalar.copy(out=gate_rows[0:1, 4:8], in_=tile_major[0:1, 4:8])
 
         def bias(copy, q):
             blend_bias(*divmod(q, TILES))
             start_acc(copy, *divmod(q, TILES))
 
-        transpose_x(0)
-        group_x(on_vector, 0)
-        transpose_x(1)
-        group_x(on_scalar, 1)
+        def x_pair(a, first_copy=on_scalar):
+            transpose_x(2 * a)
+            group_x(first_copy, 2 * a)
+            transpose_x(2 * a + 1)
+            group_x(on_scalar, 2 * a + 1)
+
         group_w(on_vector, 0, 0, 0, N_TILE)
         bias(on_scalar, 0)
-        bias(on_scalar, 1)
-        quantize_x(0)
+        bias(on_vector, 1)
         quantize_w(0, 0, 1)
-        for j in range(2, 4):
-            transpose_x(j)
-            group_x(on_scalar, j)
-        group_w(on_vector, 0, 1, 0, N_TILE)
-        quantize_x(1)
-        quantize_w(0, 1, 2)
         bias(on_scalar, 2)
+        x_pair(0, on_vector)
         bias(on_scalar, 3)
-        for j in range(2):
-            mx_pass(0, j, 0)
-        for j in range(4, TILES):
-            transpose_x(j)
-            group_x(on_scalar, j)
-            if j == 5:
-                for j2 in range(2):
-                    mx_pass(0, j2, 1)
-        project(0, 2)
-        project(0, 3)
-        blend(0, 0)
-        quantize_x(2)
-        blend(0, 1)
-        quantize_x(3)
-        group_w(on_vector, 1, 0, 0, N_TILE)
+        x_pair(1)
+        group_w(on_vector, 0, 1, 0, N_TILE)
+        quantize_x(0)
+        quantize_w(0, 1, 2)
+        quantize_x(1)
+        x_pair(2)
         bias(on_scalar, 4)
+        project(0, 0)
+        x_pair(3)
         bias(on_scalar, 5)
+        for j in range(1, 4):
+            project(0, j)
+        quantize_x(2)
+        group_w(on_vector, 1, 0, 0, N_TILE)
         group_w(on_scalar, 1, 1, 0, N_TILE)
-        project(0, 4)
-        project(0, 5)
-        bias(on_scalar, 6)
-        project(0, 6)
-        bias(on_scalar, 7)
-        blend(0, 2)
-        project(0, 7)
-        blend(0, 3)
+        blend(0, 0)
+        quantize_x(3)
+        blend(0, 1)
         quantize_w(1, 0, 1)
-        blend(0, 4)
-        blend(0, 5)
+        bias(on_scalar, 6)
+        bias(on_scalar, 7)
+        for j in range(4, TILES):
+            project(0, j)
+        blend(0, 2)
+        blend(0, 3)
         quantize_w(1, 1, 2)
-        blend(0, 6)
-        blend(0, 7)
+        blend(0, 4)
         group_w(on_scalar, 2, 0, 0, N_TILE)
-        for q in range(TILES, 4 + LEAD):
-            bias(on_scalar, q)
+        group_w(on_vector, 2, 1, 0, N_TILE)
+        blend(0, 5)
+        blend(0, 6)
+        quantize_w(2, 0, PASSES)
+        blend(0, 7)
+        for j in range(LAG):
+            if j < LEAD:
+                bias(on_scalar, TILES + j)
+            project(1, j)
+            blend(1, j)
+        group_w(on_scalar, 3, 0, 0, N_TILE)
 
-        for h in range(1, CHUNKS):
-            for j in range(TILES):
-                q = 4 * h + LEAD + j // 2
-                if j % 2 == 0 and q < STAGES * TILES:
-                    bias(on_scalar, q)
-                project(h, j)
-                blend(h, j)
-                if h + 1 < CHUNKS:
-                    if j == 0:
-                        group_w(on_scalar, h + 1, 1, VECTOR_COLS, N_TILE)
-                    if j == 1:
-                        group_w(on_vector, h + 1, 1, 0, VECTOR_COLS)
-                    if j == QJ:
-                        quantize_w(h + 1, 0, PASSES)
-                if j in (2, 4) and h + 2 < CHUNKS:
-                    group_w(on_scalar, h + 2, 0, (j - 2) * 128, j * 128)
+        tiles = STAGES * TILES
+        for m in range(TILES, tiles + LAG):
+            c, step = divmod(m + AHEAD, LAG)
+            if m + LEAD < tiles:
+                bias(on_scalar, m + LEAD)
+            if c < CHUNKS and c > 2:
+                if step == 0:
+                    group_w(on_scalar, c, 1, VECTOR_COLS, N_TILE)
+            if c + 1 < CHUNKS and step in (1, 2):
+                group_w(on_scalar, c + 1, 0, (step - 1) * 256, step * 256)
+            if m < tiles:
+                project(2 * (m // TILES), m % TILES)
+                blend(2 * (m // TILES), m % TILES)
+            if c < CHUNKS and c > 2 and step == 0:
+                group_w(on_vector, c, 1, 0, VECTOR_COLS)
+            project(2 * ((m - LAG) // TILES) + 1, (m - LAG) % TILES)
+            blend(2 * ((m - LAG) // TILES) + 1, (m - LAG) % TILES)
+            if c < CHUNKS and c > 2 and step == QS:
+                quantize_w(c, 0, PASSES)

@@ -74,10 +74,10 @@ def tile_reasoningmultiheadattention_pa_kernel(
         def out_cols(s):
             return slice((s % HALVES) * N_TILE, (s % HALVES + 1) * N_TILE)
 
-        def load_biases(queue, o):
+        def load_biases(o):
             plain, gated = biases[o]
-            queue.dma_start(out=bias_rows[o][0:1, :], in_=gated.partition_broadcast(1))
-            queue.dma_start(out=bias_rows[o][32:96:32, :], in_=plain.partition_broadcast(2))
+            nc.sync.dma_start(out=bias_rows[o][0:1, :], in_=gated.partition_broadcast(1))
+            nc.sync.dma_start(out=bias_rows[o][32:96:32, :], in_=plain.partition_broadcast(2))
 
         def load_x(a):
             nc.sync.dma_start(out=x_raw[a][:], in_=x_rows[:, 2 * a : 2 * a + 2, :])
@@ -175,24 +175,21 @@ def tile_reasoningmultiheadattention_pa_kernel(
         on_vector = nc.vector.tensor_copy
         on_scalar = nc.scalar.copy
 
-        for o in range(2):
-            nc.vector.memset(bias_rows[o][:], 0.0)
-        make_identity(nc, ident[:])
+        nc.gpsimd.memset(bias_rows[0][:].bitcast(U32), 0)
         nc.gpsimd.memset(gate_rows[:], 1.0)
+        make_identity(nc, ident[:])
         nc.scalar.dma_start(out=gate_raw[0:128:64, :], in_=gate.partition_broadcast(2))
         nc.scalar.dma_start(out=gate_col_raw[:], in_=gate.rearrange("(p j) -> p j", j=TILES))
-        load_biases(nc.scalar, 0)
         load_w(0, 0)
+        load_biases(0)
         load_x(0)
         load_x(1)
         load_w(0, 1)
         load_x(2)
         load_x(3)
-        for h in range(1, CHUNKS):
+        for h in range(1, 3):
             for g in range(PASSES):
                 load_w(h, g)
-            if h == 1:
-                load_biases(nc.sync, 1)
 
         nc.scalar.activation(out=one_minus_gate[:], in_=gate_col_raw[:], func=COPY, scale=-1.0, bias=1.0)
         tile_major = gate_raw[:].rearrange("p (m j) -> p j m", j=TILES)
@@ -212,9 +209,14 @@ def tile_reasoningmultiheadattention_pa_kernel(
             group_x(on_scalar, 2 * a + 1)
 
         group_w(on_vector, 0, 0, 0, N_TILE)
+        nc.vector.memset(bias_rows[1][:], 0.0)
         bias(on_scalar, 0)
         bias(on_vector, 1)
         quantize_w(0, 0, 1)
+        load_biases(1)
+        for h in range(3, CHUNKS):
+            for g in range(PASSES):
+                load_w(h, g)
         bias(on_scalar, 2)
         x_pair(0, on_vector)
         bias(on_scalar, 3)

@@ -22,82 +22,99 @@ PACK = 4
 K_PASS = P * PACK
 PASSES = HID // K_PASS
 N_TILE = 512
-TILES = TOKENS // P
+TOKEN_TILES = TOKENS // P
 HALVES = DQ // N_TILE
 STAGES = 2 * HALVES
 CHUNKS = 2 * STAGES
-VECTOR_COLS = 160
-LEAD = 3
-LAG = 4
-AHEAD = 4
-QS = 1
-OFF_VECTOR = ((6, 4), (6, 5), (6, 6), (6, 7))
+OUT_TILES = STAGES * TOKEN_TILES
+PLAIN, GATED = 0, 1
+
+ROW_GATE, ROW_ONE, ROW_MINUS_GATE = 0, 32, 64
+
+LAG = TOKEN_TILES // 2
+BIAS_LEAD = 3
+VECTOR_COLS = 288
+GPSIMD_COLS = 256
 
 
 def tile_reasoningmultiheadattention_pa_kernel(
     tc, x, reasoning_mask, Wq, bq, Wk, bk, Wqr, bqr, Wkr, bkr, out_0, out_1
 ):
     nc = tc.nc
-    x_rows = x.rearrange("b s k -> (b s) k").rearrange("(p j) k -> p j k", j=TILES)
+    x_rows = x.rearrange("b s k -> (b s) k").rearrange("(p j) k -> p j k", j=TOKEN_TILES)
     gate = reasoning_mask.rearrange("b s u v -> (b s u v)")
     out_rows = [
-        o.rearrange("b s h d -> (b s) (h d)").rearrange("(p j) n -> p j n", j=TILES)
-        for o in (out_0, out_1)
+        out.rearrange("b s h d -> (b s) (h d)").rearrange("(p j) n -> p j n", j=TOKEN_TILES)
+        for out in (out_0, out_1)
     ]
     weights = [(Wq, Wqr), (Wk, Wkr)]
     biases = [(bq, bqr), (bk, bkr)]
+    on_vector = nc.vector.tensor_copy
+    on_scalar = nc.scalar.copy
 
     with ExitStack() as ctx:
         keep = ctx.enter_context(tc.tile_pool(name="keep", bufs=1))
-        x_stage = ctx.enter_context(tc.tile_pool(name="x_stage", bufs=3))
-        w_stage = ctx.enter_context(tc.tile_pool(name="w_stage", bufs=4))
+        stage_pool = ctx.enter_context(tc.tile_pool(name="x_stage", bufs=3))
+        chunk_pool = ctx.enter_context(tc.tile_pool(name="w_stage", bufs=4))
         acc_pool = ctx.enter_context(tc.tile_pool(name="acc", bufs=24))
         psum = ctx.enter_context(tc.psum_pool(name="psum", bufs=8))
         ctx.enter_context(tc.manual_schedule())
 
         ident = keep.tile([P, P], F32, name="ident")
         gate_raw = keep.tile([P, TOKENS], BF16, name="gate_raw")
-        gate_rows = keep.tile([P, TILES, P], BF16, name="gate_rows")
-        gate_col_raw = keep.tile([P, TILES], BF16, name="gate_col_raw")
-        gate_col = keep.tile([P, TILES], F32, name="gate_col")
-        one_minus_gate = keep.tile([P, TILES], F32, name="one_minus_gate")
+        gate_rows = keep.tile([P, TOKEN_TILES, P], BF16, name="gate_rows")
+        gate_col_raw = keep.tile([P, TOKEN_TILES], BF16, name="gate_col_raw")
+        gate_col = keep.tile([P, TOKEN_TILES], F32, name="gate_col")
+        one_minus_gate = keep.tile([P, TOKEN_TILES], F32, name="one_minus_gate")
         bias_rows = [keep.tile([P, DQ], BF16, name="bias_rows%d" % o) for o in range(2)]
-        x_raw = [keep.tile([P, 2, HID], BF16, name="x_raw%d" % a) for a in range(TILES // 2)]
-        x_codes = [keep.tile([P, 2 * PASSES * P], U32, name="x_codes%d" % a, align_bytes=64) for a in range(TILES // 2)]
-        x_scales = [keep.tile([P, 2 * PASSES * P], U8, name="x_scales%d" % a, align_bytes=64) for a in range(TILES // 2)]
+        pairs = range(TOKEN_TILES // 2)
+        x_raw = [keep.tile([P, 2, HID], BF16, name="x_raw%d" % a) for a in pairs]
+        x_codes = [keep.tile([P, 2 * PASSES * P], U32, name="x_codes%d" % a, align_bytes=64) for a in pairs]
+        x_scales = [keep.tile([P, 2 * PASSES * P], U8, name="x_scales%d" % a, align_bytes=64) for a in pairs]
         w_raw = [
-            [keep.tile([P, PACK, N_TILE], BF16, name="w_raw%d_%d" % (h, g)) for g in range(PASSES)]
-            for h in range(CHUNKS)
+            [keep.tile([P, PACK, N_TILE], BF16, name="w_raw%d_%d" % (c, g)) for g in range(PASSES)]
+            for c in range(CHUNKS)
         ]
-        x_grouped, w_grouped, w_codes, w_scales, acc, banks, x_banks, bias_banks = {}, {}, {}, {}, {}, {}, {}, {}
+        x_grouped, w_grouped, w_codes, w_scales = {}, {}, {}, {}
+        acc, bias_bank, mx_bank = {}, {}, {}
 
-        def out_cols(s):
+        def stage_cols(s):
             return slice((s % HALVES) * N_TILE, (s % HALVES + 1) * N_TILE)
 
         def load_biases(o):
             plain, gated = biases[o]
-            nc.sync.dma_start(out=bias_rows[o][0:1, :], in_=gated.partition_broadcast(1))
-            nc.sync.dma_start(out=bias_rows[o][32:96:32, :], in_=plain.partition_broadcast(2))
+            rows = bias_rows[o]
+            nc.sync.dma_start(out=rows[ROW_GATE : ROW_GATE + 1, :], in_=gated.partition_broadcast(1))
+            nc.sync.dma_start(out=rows[ROW_ONE : ROW_MINUS_GATE + 32 : 32, :], in_=plain.partition_broadcast(2))
 
         def load_x(a):
             nc.sync.dma_start(out=x_raw[a][:], in_=x_rows[:, 2 * a : 2 * a + 2, :])
 
-        def load_w(h, g):
-            s = h // 2
-            rows = weights[s // HALVES][h % 2][g * K_PASS : (g + 1) * K_PASS, out_cols(s)]
-            nc.sync.dma_start(out=w_raw[h][g][:], in_=rows.rearrange("(p t) n -> p t n", t=PACK))
+        def load_w(c, g):
+            s, which = divmod(c, 2)
+            rows = weights[s // HALVES][which][g * K_PASS : (g + 1) * K_PASS, stage_cols(s)]
+            nc.sync.dma_start(out=w_raw[c][g][:], in_=rows.rearrange("(p t) n -> p t n", t=PACK))
 
-        def transpose_x(j):
-            x_banks[j] = psum.tile([P, PASSES, 2, P], F32, name="bank")
-            words = x_raw[j // 2][:, j % 2, :].bitcast(F32)
+        def load_chunks(first, last):
+            for c in range(first, last):
+                for g in range(PASSES):
+                    load_w(c, g)
+
+        def turn_x(copy, j):
+            a, i = divmod(j, 2)
+            bank = psum.tile([P, PASSES, 2, P], F32, name="bank")
+            words = x_raw[a][:, i, :].bitcast(F32)
+            per_pass = K_PASS // 2
             for g in range(PASSES):
                 for u in range(2):
-                    nc.tensor.transpose(x_banks[j][:, g, u, :], words[:, 256 * g + u : 256 * (g + 1) : 2], ident[:])
+                    nc.tensor.transpose(bank[:, g, u, :], words[:, per_pass * g + u : per_pass * (g + 1) : 2], ident[:])
+            if i == 0:
+                x_grouped[a] = stage_pool.tile([P, 2, PASSES, P, PACK], BF16, name="x_grouped", align_bytes=64)
+            copy(out=x_grouped[a][:, i].bitcast(F32), in_=bank[:].rearrange("p g u r -> p g r u"))
 
-        def group_x(copy, j):
-            if j % 2 == 0:
-                x_grouped[j // 2] = x_stage.tile([P, 2, PASSES, P, PACK], BF16, name="x_grouped", align_bytes=64)
-            copy(out=x_grouped[j // 2][:, j % 2].bitcast(F32), in_=x_banks[j][:].rearrange("p g u r -> p g r u"))
+        def turn_x_pair(a, first_copy=on_scalar):
+            turn_x(first_copy, 2 * a)
+            turn_x(on_scalar, 2 * a + 1)
 
         def quantize_x(a):
             nc.vector.quantize_mx(
@@ -106,80 +123,90 @@ def tile_reasoningmultiheadattention_pa_kernel(
                 in_=x_grouped[a][:].rearrange("p i g r t -> p (i g r t)"),
             )
 
-        def group_w(copy, h, g, n0, n1):
-            if h not in w_grouped:
-                w_grouped[h] = w_stage.tile([P, PASSES, N_TILE, PACK], BF16, name="w_grouped", align_bytes=64)
+        def group_w(copy, c, g, n0=0, n1=N_TILE):
+            if c not in w_grouped:
+                w_grouped[c] = chunk_pool.tile([P, PASSES, N_TILE, PACK], BF16, name="w_grouped", align_bytes=64)
             copy(
-                out=w_grouped[h][:, g, n0:n1, :].rearrange("p (c i) t -> p c t i", i=4),
-                in_=w_raw[h][g][:, :, n0:n1].rearrange("p t (c i) -> p c t i", i=4),
+                out=w_grouped[c][:, g, n0:n1, :].rearrange("p (n i) t -> p n t i", i=4),
+                in_=w_raw[c][g][:, :, n0:n1].rearrange("p t (n i) -> p n t i", i=4),
             )
 
-        def quantize_w(h, g0, g1):
-            if h not in w_codes:
-                w_codes[h] = w_stage.tile([P, PASSES * N_TILE], U32, name="w_codes", align_bytes=64)
-                w_scales[h] = w_stage.tile([P, PASSES * N_TILE], U8, name="w_scales", align_bytes=64)
+        def quantize_w(c, g0=0, g1=PASSES):
+            if c not in w_codes:
+                w_codes[c] = chunk_pool.tile([P, PASSES * N_TILE], U32, name="w_codes", align_bytes=64)
+                w_scales[c] = chunk_pool.tile([P, PASSES * N_TILE], U8, name="w_scales", align_bytes=64)
             cols = slice(g0 * N_TILE, g1 * N_TILE)
             nc.vector.quantize_mx(
-                out=w_codes[h][:, cols].bitcast(E5M2X4),
-                scales=w_scales[h][:, cols],
-                in_=w_grouped[h][:, g0:g1].rearrange("p g n t -> p (g n t)"),
+                out=w_codes[c][:, cols].bitcast(E5M2X4),
+                scales=w_scales[c][:, cols],
+                in_=w_grouped[c][:, g0:g1].rearrange("p g n t -> p (g n t)"),
             )
 
-        def blend_bias(s, j):
-            bias_banks[s, j] = psum.tile([P, N_TILE], F32, name="bank")
+        def multiply_bias(m):
+            s, j = divmod(m, TOKEN_TILES)
+            bias_bank[m] = psum.tile([P, N_TILE], F32, name="bank")
             nc.tensor.matmul(
-                out=bias_banks[s, j][:],
+                out=bias_bank[m][:],
                 lhsT=gate_rows[:, j, :],
-                rhs=bias_rows[s // HALVES][:, out_cols(s)],
+                rhs=bias_rows[s // HALVES][:, stage_cols(s)],
                 start=True,
                 stop=True,
             )
 
-        def start_acc(copy, s, j):
-            acc[s, j] = acc_pool.tile([P, N_TILE], F32, name="acc")
-            copy(out=acc[s, j][:], in_=bias_banks[s, j][:])
+        def start_acc(m, copy=on_scalar):
+            acc[m] = acc_pool.tile([P, N_TILE], F32, name="acc")
+            copy(out=acc[m][:], in_=bias_bank[m][:])
 
-        def mx_pass(h, j, g):
-            if g == 0:
-                banks[h, j] = psum.tile([P, N_TILE], F32, name="bank")
-            x_cols = slice(((j % 2) * PASSES + g) * P, ((j % 2) * PASSES + g + 1) * P)
-            w_cols = slice(g * N_TILE, (g + 1) * N_TILE)
-            nc.tensor.matmul_mx(
-                out=banks[h, j][:],
-                lhsT=x_codes[j // 2][:, x_cols].bitcast(E5M2X4),
-                lhsT_scale=x_scales[j // 2][:, x_cols],
-                rhs=w_codes[h][:, w_cols].bitcast(E5M2X4),
-                rhs_scale=w_scales[h][:, w_cols],
-                start=(g == 0),
-                stop=(g == PASSES - 1),
+        def make_bias(m, copy=on_scalar):
+            multiply_bias(m)
+            start_acc(m, copy)
+
+        def project(m, which):
+            s, j = divmod(m, TOKEN_TILES)
+            a, i = divmod(j, 2)
+            c = 2 * s + which
+            mx_bank[m, which] = psum.tile([P, N_TILE], F32, name="bank")
+            for g in range(PASSES):
+                x_cols = slice((i * PASSES + g) * P, (i * PASSES + g + 1) * P)
+                w_cols = slice(g * N_TILE, (g + 1) * N_TILE)
+                nc.tensor.matmul_mx(
+                    out=mx_bank[m, which][:],
+                    lhsT=x_codes[a][:, x_cols].bitcast(E5M2X4),
+                    lhsT_scale=x_scales[a][:, x_cols],
+                    rhs=w_codes[c][:, w_cols].bitcast(E5M2X4),
+                    rhs_scale=w_scales[c][:, w_cols],
+                    start=(g == 0),
+                    stop=(g == PASSES - 1),
+                )
+
+        def gate_factor(m, which):
+            j = m % TOKEN_TILES
+            return (one_minus_gate, gate_col)[which][:, j : j + 1]
+
+        def blend(m, which):
+            nc.vector.scalar_tensor_tensor(
+                out=acc[m][:], in0=mx_bank[m, which][:], scalar=gate_factor(m, which), in1=acc[m][:], op0=MULT, op1=ADD
             )
 
-        def project(h, j):
-            for g in range(PASSES):
-                mx_pass(h, j, g)
+        def blend_off_vector(m):
+            scaled = stage_pool.tile([P, N_TILE], F32, name="scaled")
+            nc.scalar.activation(out=scaled[:], in_=mx_bank[m, PLAIN][:], func=COPY, scale=gate_factor(m, PLAIN))
+            for n0 in range(0, N_TILE, GPSIMD_COLS):
+                cols = slice(n0, n0 + GPSIMD_COLS)
+                nc.gpsimd.tensor_tensor(out=acc[m][:, cols], in0=acc[m][:, cols], in1=scaled[:, cols], op=ADD)
 
-        def blend(h, j):
-            s = h // 2
-            factor = (one_minus_gate, gate_col)[h % 2][:, j : j + 1]
-            if (h, j) in OFF_VECTOR:
-                scaled = x_stage.tile([P, N_TILE], F32, name="scaled", bufs=3)
-                nc.scalar.activation(out=scaled[:], in_=banks[h, j][:], func=COPY, scale=factor)
-                nc.gpsimd.tensor_tensor(out=acc[s, j][:], in0=acc[s, j][:], in1=scaled[:], op=ADD)
-            else:
-                nc.vector.scalar_tensor_tensor(
-                    out=acc[s, j][:], in0=banks[h, j][:], scalar=factor, in1=acc[s, j][:], op0=MULT, op1=ADD
-                )
-            if h % 2 == 1:
-                nc.sync.dma_start(out=out_rows[s // HALVES][:, j, out_cols(s)], in_=acc[s, j][:])
-
-        on_vector = nc.vector.tensor_copy
-        on_scalar = nc.scalar.copy
+        def finish(m):
+            s, j = divmod(m, TOKEN_TILES)
+            project(m, GATED)
+            blend(m, GATED)
+            nc.sync.dma_start(out=out_rows[s // HALVES][:, j, stage_cols(s)], in_=acc[m][:])
 
         nc.gpsimd.memset(bias_rows[0][:].bitcast(U32), 0)
-        nc.gpsimd.memset(gate_rows[:], 1.0)
         make_identity(nc, ident[:])
-        nc.scalar.dma_start(out=gate_raw[0:128:64, :], in_=gate.partition_broadcast(2))
-        nc.scalar.dma_start(out=gate_col_raw[:], in_=gate.rearrange("(p j) -> p j", j=TILES))
+        nc.gpsimd.memset(gate_rows[:], 1.0)
+
+        nc.scalar.dma_start(out=gate_raw[ROW_GATE:P:ROW_MINUS_GATE, :], in_=gate.partition_broadcast(2))
+        nc.scalar.dma_start(out=gate_col_raw[:], in_=gate.rearrange("(p j) -> p j", j=TOKEN_TILES))
         load_w(0, 0)
         load_biases(0)
         load_x(0)
@@ -187,95 +214,87 @@ def tile_reasoningmultiheadattention_pa_kernel(
         load_w(0, 1)
         load_x(2)
         load_x(3)
-        for h in range(1, 3):
-            for g in range(PASSES):
-                load_w(h, g)
+        load_chunks(1, 3)
 
         nc.scalar.activation(out=one_minus_gate[:], in_=gate_col_raw[:], func=COPY, scale=-1.0, bias=1.0)
-        tile_major = gate_raw[:].rearrange("p (m j) -> p j m", j=TILES)
-        nc.scalar.copy(out=gate_rows[0:1, 0:4], in_=tile_major[0:1, 0:4])
-        nc.vector.tensor_scalar(out=gate_rows[64:65], in0=tile_major[64:65], scalar1=-1.0, scalar2=None, op0=MULT)
-        nc.vector.tensor_copy(out=gate_col[:], in_=gate_col_raw[:])
-        nc.scalar.copy(out=gate_rows[0:1, 4:8], in_=tile_major[0:1, 4:8])
+        by_tile = gate_raw[:].rearrange("p (r j) -> p j r", j=TOKEN_TILES)
+        plus, minus = slice(ROW_GATE, ROW_GATE + 1), slice(ROW_MINUS_GATE, ROW_MINUS_GATE + 1)
+        half = TOKEN_TILES // 2
+        on_scalar(out=gate_rows[plus, :half], in_=by_tile[plus, :half])
+        nc.vector.tensor_scalar(out=gate_rows[minus], in0=by_tile[minus], scalar1=-1.0, scalar2=None, op0=MULT)
+        on_vector(out=gate_col[:], in_=gate_col_raw[:])
+        on_scalar(out=gate_rows[plus, half:], in_=by_tile[plus, half:])
 
-        def bias(copy, q):
-            blend_bias(*divmod(q, TILES))
-            start_acc(copy, *divmod(q, TILES))
-
-        def x_pair(a, first_copy=on_scalar):
-            transpose_x(2 * a)
-            group_x(first_copy, 2 * a)
-            transpose_x(2 * a + 1)
-            group_x(on_scalar, 2 * a + 1)
-
-        group_w(on_vector, 0, 0, 0, N_TILE)
+        group_w(on_vector, 0, 0)
         nc.vector.memset(bias_rows[1][:], 0.0)
-        bias(on_scalar, 0)
-        bias(on_vector, 1)
+        make_bias(0)
+        make_bias(1, on_vector)
         quantize_w(0, 0, 1)
         load_biases(1)
-        for h in range(3, CHUNKS):
-            for g in range(PASSES):
-                load_w(h, g)
-        bias(on_scalar, 2)
-        x_pair(0, on_vector)
-        bias(on_scalar, 3)
-        x_pair(1)
-        group_w(on_vector, 0, 1, 0, N_TILE)
+        load_chunks(3, CHUNKS)
+        make_bias(2)
+        turn_x_pair(0, on_vector)
+        multiply_bias(3)
+        multiply_bias(4)
+        start_acc(3)
+        turn_x_pair(1)
+        start_acc(4)
+        multiply_bias(5)
+        multiply_bias(6)
+        group_w(on_vector, 0, 1)
         quantize_x(0)
         quantize_w(0, 1, 2)
         quantize_x(1)
-        x_pair(2)
-        bias(on_scalar, 4)
-        project(0, 0)
-        x_pair(3)
-        bias(on_scalar, 5)
-        for j in range(1, 4):
-            project(0, j)
-        quantize_x(2)
-        group_w(on_vector, 1, 0, 0, N_TILE)
-        group_w(on_scalar, 1, 1, 0, N_TILE)
-        blend(0, 0)
-        quantize_x(3)
-        blend(0, 1)
-        quantize_w(1, 0, 1)
-        bias(on_scalar, 6)
-        bias(on_scalar, 7)
-        for j in range(4, TILES):
-            project(0, j)
-        blend(0, 2)
-        blend(0, 3)
-        quantize_w(1, 1, 2)
-        blend(0, 4)
-        group_w(on_scalar, 2, 0, 0, N_TILE)
-        group_w(on_vector, 2, 1, 0, N_TILE)
-        blend(0, 5)
-        blend(0, 6)
-        quantize_w(2, 0, PASSES)
-        blend(0, 7)
-        for j in range(LAG):
-            if j < LEAD:
-                bias(on_scalar, TILES + j)
-            project(1, j)
-            blend(1, j)
-        group_w(on_scalar, 3, 0, 0, N_TILE)
+        turn_x_pair(2)
+        project(0, PLAIN)
+        start_acc(5)
+        turn_x_pair(3)
+        start_acc(6)
 
-        tiles = STAGES * TILES
-        for m in range(TILES, tiles + LAG):
-            c, step = divmod(m + AHEAD, LAG)
-            if m + LEAD < tiles:
-                bias(on_scalar, m + LEAD)
-            if c < CHUNKS and c > 2:
-                if step == 0:
-                    group_w(on_scalar, c, 1, VECTOR_COLS, N_TILE)
-            if c + 1 < CHUNKS and step in (1, 2):
-                group_w(on_scalar, c + 1, 0, (step - 1) * 256, step * 256)
-            if m < tiles:
-                project(2 * (m // TILES), m % TILES)
-                blend(2 * (m // TILES), m % TILES)
-            if c < CHUNKS and c > 2 and step == 0:
+        for m in range(1, 4):
+            project(m, PLAIN)
+        group_w(on_vector, 1, 0)
+        group_w(on_scalar, 1, 1)
+        quantize_x(2)
+        blend(0, PLAIN)
+        quantize_w(1, 0, 1)
+        blend(1, PLAIN)
+        quantize_x(3)
+        make_bias(7)
+        for m in range(4, TOKEN_TILES):
+            project(m, PLAIN)
+        blend(2, PLAIN)
+        blend(3, PLAIN)
+        quantize_w(1, 1, 2)
+        blend(4, PLAIN)
+        group_w(on_scalar, 2, 0)
+        group_w(on_vector, 2, 1)
+        blend(5, PLAIN)
+        blend(6, PLAIN)
+        quantize_w(2)
+        blend(7, PLAIN)
+        for m in range(LAG):
+            if m < BIAS_LEAD:
+                make_bias(TOKEN_TILES + m)
+            finish(m)
+        group_w(on_scalar, 3, 0)
+
+        for m in range(TOKEN_TILES, OUT_TILES + LAG):
+            c, phase = divmod(m + LAG, LAG)
+            if m + BIAS_LEAD < OUT_TILES:
+                make_bias(m + BIAS_LEAD)
+            if c < CHUNKS and phase == 0:
+                group_w(on_scalar, c, 1, VECTOR_COLS, N_TILE)
+            if c + 1 < CHUNKS and phase in (1, 2):
+                group_w(on_scalar, c + 1, 0, (phase - 1) * N_TILE // 2, phase * N_TILE // 2)
+            if m < OUT_TILES:
+                project(m, PLAIN)
+                if phase == 1 or m >= OUT_TILES - LAG:
+                    blend_off_vector(m)
+                else:
+                    blend(m, PLAIN)
+            if c < CHUNKS and phase == 0:
                 group_w(on_vector, c, 1, 0, VECTOR_COLS)
-            project(2 * ((m - LAG) // TILES) + 1, (m - LAG) % TILES)
-            blend(2 * ((m - LAG) // TILES) + 1, (m - LAG) % TILES)
-            if c < CHUNKS and c > 2 and step == QS:
-                quantize_w(c, 0, PASSES)
+            finish(m - LAG)
+            if c < CHUNKS and phase == 1:
+                quantize_w(c)

from contextlib import ExitStack

import concourse.mybir as mybir
from concourse.masks import make_identity

B, S, HID, NH, DH = 4, 256, 1024, 16, 64
TOKENS = B * S
DQ = NH * DH
FLOPS = 4 * 2 * TOKENS * HID * DQ

F32 = mybir.dt.float32
BF16 = mybir.dt.bfloat16
U32 = mybir.dt.uint32
U8 = mybir.dt.uint8
E5M2X4 = mybir.dt.float8_e5m2_x4
MULT = mybir.AluOpType.mult
ADD = mybir.AluOpType.add
COPY = mybir.ActivationFunctionType.Copy

P = 128
PACK = 4
K_PASS = P * PACK
PASSES = HID // K_PASS
N_TILE = 512
TOKEN_TILES = TOKENS // P
HALVES = DQ // N_TILE
STAGES = 2 * HALVES
CHUNKS = 2 * STAGES
OUT_TILES = STAGES * TOKEN_TILES
PLAIN, GATED = 0, 1

ROW_GATE, ROW_ONE, ROW_MINUS_GATE = 0, 32, 64

LAG = TOKEN_TILES // 2
BIAS_LEAD = 3
VECTOR_COLS = 288
GPSIMD_COLS = 256


def tile_reasoningmultiheadattention_pa_kernel(
    tc, x, reasoning_mask, Wq, bq, Wk, bk, Wqr, bqr, Wkr, bkr, out_0, out_1
):
    nc = tc.nc
    x_rows = x.rearrange("b s k -> (b s) k").rearrange("(p j) k -> p j k", j=TOKEN_TILES)
    gate = reasoning_mask.rearrange("b s u v -> (b s u v)")
    out_rows = [
        out.rearrange("b s h d -> (b s) (h d)").rearrange("(p j) n -> p j n", j=TOKEN_TILES)
        for out in (out_0, out_1)
    ]
    weights = [(Wq, Wqr), (Wk, Wkr)]
    biases = [(bq, bqr), (bk, bkr)]
    on_vector = nc.vector.tensor_copy
    on_scalar = nc.scalar.copy

    with ExitStack() as ctx:
        keep = ctx.enter_context(tc.tile_pool(name="keep", bufs=1))
        stage_pool = ctx.enter_context(tc.tile_pool(name="x_stage", bufs=3))
        chunk_pool = ctx.enter_context(tc.tile_pool(name="w_stage", bufs=4))
        acc_pool = ctx.enter_context(tc.tile_pool(name="acc", bufs=24))
        psum = ctx.enter_context(tc.psum_pool(name="psum", bufs=8))
        ctx.enter_context(tc.manual_schedule())

        ident = keep.tile([P, P], F32, name="ident")
        gate_raw = keep.tile([P, TOKENS], BF16, name="gate_raw")
        gate_rows = keep.tile([P, TOKEN_TILES, P], BF16, name="gate_rows")
        gate_col_raw = keep.tile([P, TOKEN_TILES], BF16, name="gate_col_raw")
        gate_col = keep.tile([P, TOKEN_TILES], F32, name="gate_col")
        one_minus_gate = keep.tile([P, TOKEN_TILES], F32, name="one_minus_gate")
        bias_rows = [keep.tile([P, DQ], BF16, name="bias_rows%d" % o) for o in range(2)]
        pairs = range(TOKEN_TILES // 2)
        x_raw = [keep.tile([P, 2, HID], BF16, name="x_raw%d" % a) for a in pairs]
        x_codes = [keep.tile([P, 2 * PASSES * P], U32, name="x_codes%d" % a, align_bytes=64) for a in pairs]
        x_scales = [keep.tile([P, 2 * PASSES * P], U8, name="x_scales%d" % a, align_bytes=64) for a in pairs]
        w_raw = [
            [keep.tile([P, PACK, N_TILE], BF16, name="w_raw%d_%d" % (c, g)) for g in range(PASSES)]
            for c in range(CHUNKS)
        ]
        x_grouped, w_grouped, w_codes, w_scales = {}, {}, {}, {}
        acc, bias_bank, mx_bank = {}, {}, {}

        def stage_cols(s):
            return slice((s % HALVES) * N_TILE, (s % HALVES + 1) * N_TILE)

        def load_biases(o):
            plain, gated = biases[o]
            rows = bias_rows[o]
            nc.sync.dma_start(out=rows[ROW_GATE : ROW_GATE + 1, :], in_=gated.partition_broadcast(1))
            nc.sync.dma_start(out=rows[ROW_ONE : ROW_MINUS_GATE + 32 : 32, :], in_=plain.partition_broadcast(2))

        def load_x(a):
            nc.sync.dma_start(out=x_raw[a][:], in_=x_rows[:, 2 * a : 2 * a + 2, :])

        def load_w(c, g):
            s, which = divmod(c, 2)
            rows = weights[s // HALVES][which][g * K_PASS : (g + 1) * K_PASS, stage_cols(s)]
            nc.sync.dma_start(out=w_raw[c][g][:], in_=rows.rearrange("(p t) n -> p t n", t=PACK))

        def load_chunks(first, last):
            for c in range(first, last):
                for g in range(PASSES):
                    load_w(c, g)

        def turn_x(copy, j):
            a, i = divmod(j, 2)
            bank = psum.tile([P, PASSES, 2, P], F32, name="bank")
            words = x_raw[a][:, i, :].bitcast(F32)
            per_pass = K_PASS // 2
            for g in range(PASSES):
                for u in range(2):
                    nc.tensor.transpose(bank[:, g, u, :], words[:, per_pass * g + u : per_pass * (g + 1) : 2], ident[:])
            if i == 0:
                x_grouped[a] = stage_pool.tile([P, 2, PASSES, P, PACK], BF16, name="x_grouped", align_bytes=64)
            copy(out=x_grouped[a][:, i].bitcast(F32), in_=bank[:].rearrange("p g u r -> p g r u"))

        def turn_x_pair(a, first_copy=on_scalar):
            turn_x(first_copy, 2 * a)
            turn_x(on_scalar, 2 * a + 1)

        def quantize_x(a):
            nc.vector.quantize_mx(
                out=x_codes[a][:].bitcast(E5M2X4),
                scales=x_scales[a][:],
                in_=x_grouped[a][:].rearrange("p i g r t -> p (i g r t)"),
            )

        def group_w(copy, c, g, n0=0, n1=N_TILE):
            if c not in w_grouped:
                w_grouped[c] = chunk_pool.tile([P, PASSES, N_TILE, PACK], BF16, name="w_grouped", align_bytes=64)
            copy(
                out=w_grouped[c][:, g, n0:n1, :].rearrange("p (n i) t -> p n t i", i=4),
                in_=w_raw[c][g][:, :, n0:n1].rearrange("p t (n i) -> p n t i", i=4),
            )

        def quantize_w(c, g0=0, g1=PASSES):
            if c not in w_codes:
                w_codes[c] = chunk_pool.tile([P, PASSES * N_TILE], U32, name="w_codes", align_bytes=64)
                w_scales[c] = chunk_pool.tile([P, PASSES * N_TILE], U8, name="w_scales", align_bytes=64)
            cols = slice(g0 * N_TILE, g1 * N_TILE)
            nc.vector.quantize_mx(
                out=w_codes[c][:, cols].bitcast(E5M2X4),
                scales=w_scales[c][:, cols],
                in_=w_grouped[c][:, g0:g1].rearrange("p g n t -> p (g n t)"),
            )

        def multiply_bias(m):
            s, j = divmod(m, TOKEN_TILES)
            bias_bank[m] = psum.tile([P, N_TILE], F32, name="bank")
            nc.tensor.matmul(
                out=bias_bank[m][:],
                lhsT=gate_rows[:, j, :],
                rhs=bias_rows[s // HALVES][:, stage_cols(s)],
                start=True,
                stop=True,
            )

        def start_acc(m, copy=on_scalar):
            acc[m] = acc_pool.tile([P, N_TILE], F32, name="acc")
            copy(out=acc[m][:], in_=bias_bank[m][:])

        def make_bias(m, copy=on_scalar):
            multiply_bias(m)
            start_acc(m, copy)

        def project(m, which):
            s, j = divmod(m, TOKEN_TILES)
            a, i = divmod(j, 2)
            c = 2 * s + which
            mx_bank[m, which] = psum.tile([P, N_TILE], F32, name="bank")
            for g in range(PASSES):
                x_cols = slice((i * PASSES + g) * P, (i * PASSES + g + 1) * P)
                w_cols = slice(g * N_TILE, (g + 1) * N_TILE)
                nc.tensor.matmul_mx(
                    out=mx_bank[m, which][:],
                    lhsT=x_codes[a][:, x_cols].bitcast(E5M2X4),
                    lhsT_scale=x_scales[a][:, x_cols],
                    rhs=w_codes[c][:, w_cols].bitcast(E5M2X4),
                    rhs_scale=w_scales[c][:, w_cols],
                    start=(g == 0),
                    stop=(g == PASSES - 1),
                )

        def gate_factor(m, which):
            j = m % TOKEN_TILES
            return (one_minus_gate, gate_col)[which][:, j : j + 1]

        def blend(m, which):
            nc.vector.scalar_tensor_tensor(
                out=acc[m][:], in0=mx_bank[m, which][:], scalar=gate_factor(m, which), in1=acc[m][:], op0=MULT, op1=ADD
            )

        def blend_off_vector(m):
            scaled = stage_pool.tile([P, N_TILE], F32, name="scaled")
            nc.scalar.activation(out=scaled[:], in_=mx_bank[m, PLAIN][:], func=COPY, scale=gate_factor(m, PLAIN))
            for n0 in range(0, N_TILE, GPSIMD_COLS):
                cols = slice(n0, n0 + GPSIMD_COLS)
                nc.gpsimd.tensor_tensor(out=acc[m][:, cols], in0=acc[m][:, cols], in1=scaled[:, cols], op=ADD)

        def finish(m):
            s, j = divmod(m, TOKEN_TILES)
            project(m, GATED)
            blend(m, GATED)
            nc.sync.dma_start(out=out_rows[s // HALVES][:, j, stage_cols(s)], in_=acc[m][:])

        nc.gpsimd.memset(bias_rows[0][:].bitcast(U32), 0)
        make_identity(nc, ident[:])
        nc.gpsimd.memset(gate_rows[:], 1.0)

        nc.scalar.dma_start(out=gate_raw[ROW_GATE:P:ROW_MINUS_GATE, :], in_=gate.partition_broadcast(2))
        nc.scalar.dma_start(out=gate_col_raw[:], in_=gate.rearrange("(p j) -> p j", j=TOKEN_TILES))
        load_w(0, 0)
        load_biases(0)
        load_x(0)
        load_x(1)
        load_w(0, 1)
        load_x(2)
        load_x(3)
        load_chunks(1, 3)

        nc.scalar.activation(out=one_minus_gate[:], in_=gate_col_raw[:], func=COPY, scale=-1.0, bias=1.0)
        by_tile = gate_raw[:].rearrange("p (r j) -> p j r", j=TOKEN_TILES)
        plus, minus = slice(ROW_GATE, ROW_GATE + 1), slice(ROW_MINUS_GATE, ROW_MINUS_GATE + 1)
        half = TOKEN_TILES // 2
        on_scalar(out=gate_rows[plus, :half], in_=by_tile[plus, :half])
        nc.vector.tensor_scalar(out=gate_rows[minus], in0=by_tile[minus], scalar1=-1.0, scalar2=None, op0=MULT)
        on_vector(out=gate_col[:], in_=gate_col_raw[:])
        on_scalar(out=gate_rows[plus, half:], in_=by_tile[plus, half:])

        group_w(on_vector, 0, 0)
        nc.vector.memset(bias_rows[1][:], 0.0)
        make_bias(0)
        make_bias(1, on_vector)
        quantize_w(0, 0, 1)
        load_biases(1)
        load_chunks(3, CHUNKS)
        make_bias(2)
        turn_x_pair(0, on_vector)
        multiply_bias(3)
        multiply_bias(4)
        start_acc(3)
        turn_x_pair(1)
        start_acc(4)
        multiply_bias(5)
        multiply_bias(6)
        group_w(on_vector, 0, 1)
        quantize_x(0)
        quantize_w(0, 1, 2)
        quantize_x(1)
        turn_x_pair(2)
        project(0, PLAIN)
        start_acc(5)
        turn_x_pair(3)
        start_acc(6)

        for m in range(1, 4):
            project(m, PLAIN)
        group_w(on_vector, 1, 0)
        group_w(on_scalar, 1, 1)
        quantize_x(2)
        blend(0, PLAIN)
        quantize_w(1, 0, 1)
        blend(1, PLAIN)
        quantize_x(3)
        make_bias(7)
        for m in range(4, TOKEN_TILES):
            project(m, PLAIN)
        blend(2, PLAIN)
        blend(3, PLAIN)
        quantize_w(1, 1, 2)
        blend(4, PLAIN)
        group_w(on_scalar, 2, 0)
        group_w(on_vector, 2, 1)
        blend(5, PLAIN)
        blend(6, PLAIN)
        quantize_w(2)
        blend(7, PLAIN)
        for m in range(LAG):
            if m < BIAS_LEAD:
                make_bias(TOKEN_TILES + m)
            finish(m)
        group_w(on_scalar, 3, 0)

        for m in range(TOKEN_TILES, OUT_TILES + LAG):
            c, phase = divmod(m + LAG, LAG)
            if m + BIAS_LEAD < OUT_TILES:
                make_bias(m + BIAS_LEAD)
            if c < CHUNKS and phase == 0:
                group_w(on_scalar, c, 1, VECTOR_COLS, N_TILE)
            if c + 1 < CHUNKS and phase in (1, 2):
                group_w(on_scalar, c + 1, 0, (phase - 1) * N_TILE // 2, phase * N_TILE // 2)
            if m < OUT_TILES:
                project(m, PLAIN)
                if phase == 1 or m >= OUT_TILES - LAG:
                    blend_off_vector(m)
                else:
                    blend(m, PLAIN)
            if c < CHUNKS and phase == 0:
                group_w(on_vector, c, 1, 0, VECTOR_COLS)
            finish(m - LAG)
            if c < CHUNKS and phase == 1:
                quantize_w(c)
